import numpy as np
import ml_dtypes


def mxq(x, axis, fmt="e4m3"):
    dtype, down = {"e4m3": (ml_dtypes.float8_e4m3fn, 7), "e5m2": (ml_dtypes.float8_e5m2, 14)}[fmt]
    v = np.moveaxis(np.asarray(x, np.float32).astype(ml_dtypes.bfloat16).astype(np.float64), axis, -1)
    blocks = v.reshape(v.shape[:-1] + (-1, 32))
    amax = np.abs(blocks).max(-1, keepdims=True)
    byte = np.maximum(np.where(amax > 0, np.frexp(amax)[1] - 1 + 127, 0) - down, 1)
    scale = np.exp2(byte - 127.0)
    codes = (blocks / scale).astype(np.float32).astype(dtype).astype(np.float64)
    return np.moveaxis((codes * scale).reshape(v.shape), -1, axis)


WIDE = False


def mx_kscale(k):
    if not WIDE:
        return np.ones(k)
    levels = np.array([10, -10, 5, -5, 0])
    if k % 512:
        return np.exp2(np.random.permutation(np.resize(levels, k // 32))).repeat(32)
    a = np.empty((k // 512, 16))
    for p in range(k // 512):
        a[p, :8] = np.random.permutation(np.resize(levels, 8))
        for g in range(8):
            far = levels[np.abs(levels - a[p, g]) >= 10]
            a[p, g + 8] = far[np.random.randint(len(far))]
    return np.exp2(a.ravel()).repeat(32)


BF16 = ml_dtypes.bfloat16


def bf(x):
    return np.asarray(x, np.float32).astype(BF16)


def f64(x):
    return np.asarray(x).astype(np.float64)


T, HS, WS, WT, WH, WW, NH, HD, VID_DIM, TXT_DIM, TXT_LEN = 8, 8, 16, 8, 8, 8, 8, 128, 1536, 1536, 256
EPS = 1e-6
L_VID = T * HS * WS
N_WIN = (T // WT) * (HS // WH) * (WS // WW)
WIN_LEN = WT * WH * WW
INNER = NH * HD


def rmsnorm(x, gain):
    return x * (1.0 / np.sqrt(np.mean(x * x, axis=-1, keepdims=True) + EPS)) * gain


def window_partition(x):
    x = x.reshape(T // WT, WT, HS // WH, WH, WS // WW, WW, NH, HD)
    x = x.transpose(0, 2, 4, 1, 3, 5, 6, 7)
    return x.reshape(N_WIN, WIN_LEN, NH, HD)


def setup_inputs():
    s = mx_kscale(VID_DIM)
    return {
        "vid": bf(np.random.standard_normal((L_VID, VID_DIM)) * s),
        "Wqkv_vid": bf(np.random.standard_normal((VID_DIM, 3 * INNER)) / np.sqrt(VID_DIM) / s[:, None]),
        "bqkv_vid": bf(0.1 * np.random.standard_normal(3 * INNER)),
        "q_scale_vid": bf(1.0 + 0.1 * np.random.standard_normal(HD)),
        "k_scale_vid": bf(1.0 + 0.1 * np.random.standard_normal(HD)),
    }


def reference(vid, Wqkv_vid, bqkv_vid, q_scale_vid, k_scale_vid):
    qkv = ((mxq(f64(vid), 1, "e4m3") @ mxq(f64(Wqkv_vid), 0, "e4m3")) + f64(bqkv_vid)).reshape(L_VID, 3, NH, HD)
    q = rmsnorm(qkv[:, 0], f64(q_scale_vid))
    k = rmsnorm(qkv[:, 1], f64(k_scale_vid))
    return window_partition(q), window_partition(k), window_partition(qkv[:, 2])

@@ -1,0 +1,208 @@
+from contextlib import ExitStack
+
+import concourse.mybir as mybir
+from concourse.masks import make_identity
+
+F32 = mybir.dt.float32
+BF16 = mybir.dt.bfloat16
+I32 = mybir.dt.int32
+U32 = mybir.dt.uint32
+U8 = mybir.dt.uint8
+FP8X4 = mybir.dt.float8_e4m3fn_x4
+ACT = mybir.ActivationFunctionType
+ALU = mybir.AluOpType
+
+P = 128
+PACK = 4
+K_PASS = P * PACK
+BANK = 512
+
+TOKENS = 1024
+K = 1536
+PASSES = K // K_PASS
+PARTS = 3
+PART_ORDER = (0, 2, 1)
+HEADS = 8
+HD = 128
+PART_COLS = HEADS * HD
+N_OUT = PARTS * PART_COLS
+HALVES = PART_COLS // BANK
+WINDOWS = 2
+WIN_W = 8
+PAIRS = TOKENS // (2 * P)
+EPS = 1e-6
+ROW_COLS = N_OUT + 2 * HD
+
+FLOPS = 2 * TOKENS * K * N_OUT
+
+
+def tile_naswinattention_pa_kernel(tc, vid, w_qkv, bias, q_gain, k_gain, out_q, out_k, out_v):
+    nc = tc.nc
+    outs = (out_q, out_k, out_v)
+
+    with ExitStack() as ctx:
+        consts = ctx.enter_context(tc.tile_pool(name="consts", bufs=1))
+        keep = ctx.enter_context(tc.tile_pool(name="keep", bufs=1))
+        stage_v = ctx.enter_context(tc.tile_pool(name="stage_v", bufs=2))
+        stage_w = ctx.enter_context(tc.tile_pool(name="stage_w", bufs=4))
+        results = ctx.enter_context(tc.tile_pool(name="results", bufs=6))
+        scratch = ctx.enter_context(tc.tile_pool(name="scratch", bufs=4))
+        stats = ctx.enter_context(tc.tile_pool(name="stats", bufs=8))
+        psum_t = ctx.enter_context(tc.psum_pool(name="psum_t", bufs=2))
+        psum_acc = ctx.enter_context(tc.psum_pool(name="psum_acc", bufs=6))
+
+        rows = consts.tile([P, ROW_COLS], BF16)
+        nc.vector.memset(rows[:].bitcast(I32), 0)
+
+        vid_pairs = vid.rearrange("(a j p) k -> a p j k", j=2, p=P)
+        vid_sb = [keep.tile([P, 2, K], BF16, name="vid_sb%d" % a) for a in range(PAIRS)]
+        w_rows = w_qkv.rearrange("(g p t) c -> g p t c", p=P, t=PACK)
+        w_raw = [
+            [keep.tile([P, PACK, PART_COLS], BF16, name="w_raw%d_%d" % (s, g)) for g in range(PASSES)]
+            for s in range(PARTS)
+        ]
+
+        def load_vid(a):
+            nc.sync.dma_start(out=vid_sb[a][:], in_=vid_pairs[a])
+
+        def load_weights(s):
+            for g in range(PASSES):
+                nc.sync.dma_start(out=w_raw[s][g][:], in_=w_rows[g, :, :, s * PART_COLS : (s + 1) * PART_COLS])
+
+        with tc.manual_schedule():
+            load_vid(0)
+            nc.sync.dma_start(out=rows[0:1, 0:N_OUT], in_=bias.unsqueeze(0))
+            nc.sync.dma_start(out=rows[0:1, N_OUT : N_OUT + HD], in_=q_gain.unsqueeze(0))
+            nc.sync.dma_start(out=rows[0:1, N_OUT + HD : ROW_COLS], in_=k_gain.unsqueeze(0))
+            load_weights(PART_ORDER[0])
+            for a in range(1, PAIRS):
+                load_vid(a)
+            load_weights(PART_ORDER[1])
+            load_weights(PART_ORDER[2])
+
+        ident = consts.tile([P, P], F32)
+        make_identity(nc, ident[:])
+        ones = consts.tile([P, P], BF16)
+        nc.vector.memset(ones[:], 1.0)
+        eps = consts.tile([P, 1], F32)
+        nc.vector.memset(eps[:], EPS)
+
+        spread = consts.tile([P, ROW_COLS], BF16)
+
+        def spread_columns(first, width, copy):
+            summed = psum_acc.tile([P, BANK], F32, tag="acc")
+            nc.tensor.matmul(
+                out=summed[:, :width], lhsT=ones[:], rhs=rows[:, first : first + width], start=True, stop=True
+            )
+            copy(out=spread[:, first : first + width], in_=summed[:, :width])
+
+        v_codes = [keep.tile([P, PAIRS, WINDOWS, P], U32, name="v_codes%d" % g, align_bytes=64) for g in range(PASSES)]
+        v_scales = [keep.tile([P, PAIRS, WINDOWS, P], U8, name="v_scales%d" % g, align_bytes=64) for g in range(PASSES)]
+
+        def quantise_tokens(a):
+            words = vid_sb[a][:].bitcast(F32)
+            grouped_v = stage_v.tile([P, PASSES, WINDOWS, P * PACK], BF16, align_bytes=64)
+            grouped_words = grouped_v[:].bitcast(F32)
+            for g in range(PASSES):
+                flipped = psum_t.tile([P, 2, 2 * P], F32)
+                for u in range(2):
+                    for j in range(2):
+                        nc.tensor.transpose(
+                            flipped[:, u, j * P : (j + 1) * P],
+                            words[:, j, 2 * P * g + u : 2 * P * (g + 1) : 2],
+                            ident[:],
+                        )
+                by_window = flipped[:].rearrange("p u (s n w) -> p n s w u", n=WINDOWS, w=WIN_W)
+                for n in range(WINDOWS):
+                    nc.scalar.copy(
+                        out=grouped_words[:, g, n, :].rearrange("p (s w u) -> p s w u", w=WIN_W, u=2),
+                        in_=by_window[:, n],
+                    )
+            for g in range(PASSES):
+                nc.vector.quantize_mx(
+                    out=v_codes[g][:, a].rearrange("p n c -> p (n c)").bitcast(FP8X4),
+                    scales=v_scales[g][:, a].rearrange("p n c -> p (n c)"),
+                    in_=grouped_v[:, g].rearrange("p n c -> p (n c)"),
+                )
+
+        w_codes = [keep.tile([P, PASSES, PART_COLS], U32, name="w_codes%d" % s, align_bytes=64) for s in range(PARTS)]
+        w_scales = [keep.tile([P, PASSES, PART_COLS], U8, name="w_scales%d" % s, align_bytes=64) for s in range(PARTS)]
+
+        def quantise_weights(s, g, h):
+            cols = slice(h * BANK, (h + 1) * BANK)
+            copy = nc.vector.tensor_copy if (s != PART_ORDER[-1] and h == 0) else nc.scalar.copy
+            grouped_w = stage_w.tile([P, BANK, PACK], BF16, align_bytes=64)
+            copy(
+                out=grouped_w[:].rearrange("p (c i) t -> p c t i", i=4),
+                in_=w_raw[s][g][:, :, cols].rearrange("p t (c i) -> p c t i", i=4),
+            )
+            nc.vector.quantize_mx(
+                out=w_codes[s][:, g, cols].bitcast(FP8X4),
+                scales=w_scales[s][:, g, cols],
+                in_=grouped_w[:].rearrange("p c t -> p (c t)"),
+            )
+
+        def project(s, a, n):
+            y = results.tile([P, PART_COLS], F32)
+            for h in range(HALVES):
+                cols = slice(h * BANK, (h + 1) * BANK)
+                acc = psum_acc.tile([P, BANK], F32, tag="acc")
+                for g in range(PASSES):
+                    nc.tensor.matmul_mx(
+                        out=acc[:],
+                        lhsT=v_codes[g][:, a, n, :].bitcast(FP8X4),
+                        lhsT_scale=v_scales[g][:, a, n, :],
+                        rhs=w_codes[s][:, g, cols].bitcast(FP8X4),
+                        rhs_scale=w_scales[s][:, g, cols],
+                        start=(g == 0),
+                        stop=(g == PASSES - 1),
+                    )
+                first = s * PART_COLS + h * BANK
+                nc.vector.tensor_tensor(out=y[:, cols], in0=acc[:], in1=spread[:, first : first + BANK], op=ALU.add)
+                if s < 2:
+                    gain = spread[:, N_OUT + s * HD : N_OUT + (s + 1) * HD]
+                    heads = [slice(c0, c0 + HD) for c0 in range(h * BANK, (h + 1) * BANK, HD)]
+                    squares = scratch.tile([P, BANK], BF16)
+                    sum_sq = stats.tile([P, len(heads)], F32)
+                    for i, head in enumerate(heads):
+                        nc.scalar.activation(
+                            out=squares[:, i * HD : (i + 1) * HD],
+                            in_=y[:, head],
+                            func=ACT.Square,
+                            accum_out=sum_sq[:, i : i + 1],
+                        )
+                    rstd = stats.tile([P, len(heads)], F32)
+                    nc.scalar.activation(
+                        out=rstd[:], in_=sum_sq[:], func=ACT.Abs_reciprocal_sqrt, scale=1.0 / HD, bias=eps[:]
+                    )
+                    for i, head in enumerate(heads):
+                        nc.vector.scalar_tensor_tensor(
+                            out=y[:, head],
+                            in0=y[:, head],
+                            scalar=rstd[:, i : i + 1],
+                            in1=gain,
+                            op0=ALU.mult,
+                            op1=ALU.mult,
+                        )
+            nc.sync.dma_start(out=outs[s][n, a * P : (a + 1) * P].rearrange("p h d -> p (h d)"), in_=y[:])
+
+        units = [(g, h) for g in range(PASSES) for h in range(HALVES)]
+        tiles = [(a, n) for a in range(PAIRS) for n in range(WINDOWS)]
+
+        spread_columns(N_OUT, 2 * HD, nc.vector.tensor_copy)
+        for h in range(HALVES):
+            spread_columns(PART_ORDER[0] * PART_COLS + h * BANK, BANK, nc.vector.tensor_copy)
+        quantise_tokens(0)
+        for g, h in units:
+            quantise_weights(PART_ORDER[0], g, h)
+        for a in range(1, PAIRS):
+            quantise_tokens(a)
+        for turn, s in enumerate(PART_ORDER):
+            for i, (a, n) in enumerate(tiles):
+                if turn + 1 < PARTS and i < len(units):
+                    g, h = units[i]
+                    quantise_weights(PART_ORDER[turn + 1], g, h)
+                elif turn + 1 < PARTS:
+                    h = i - len(units)
+                    spread_columns(PART_ORDER[turn + 1] * PART_COLS + h * BANK, BANK, nc.scalar.copy)
+                project(s, a, n)

@@ -31,6 +31,7 @@ WINDOWS = 2
 WIN_W = 8
 PAIRS = TOKENS // (2 * P)
 EPS = 1e-6
+SHARED_HEADS = 1
 ROW_COLS = N_OUT + 2 * HD
 
 FLOPS = 2 * TOKENS * K * N_OUT
@@ -49,7 +50,8 @@ def tile_naswinattention_pa_kernel(tc, vid, w_qkv, bias, q_gain, k_gain, out_q, 
         scratch = ctx.enter_context(tc.tile_pool(name="scratch", bufs=4))
         stats = ctx.enter_context(tc.tile_pool(name="stats", bufs=8))
         psum_t = ctx.enter_context(tc.psum_pool(name="psum_t", bufs=2))
-        psum_acc = ctx.enter_context(tc.psum_pool(name="psum_acc", bufs=6))
+        psum_acc = ctx.enter_context(tc.psum_pool(name="psum_acc", bufs=5))
+        psum_gain = ctx.enter_context(tc.psum_pool(name="psum_gain", bufs=1))
 
         rows = consts.tile([P, ROW_COLS], BF16)
         nc.vector.memset(rows[:].bitcast(I32), 0)
@@ -65,16 +67,17 @@ def tile_naswinattention_pa_kernel(tc, vid, w_qkv, bias, q_gain, k_gain, out_q, 
         def load_vid(a):
             nc.sync.dma_start(out=vid_sb[a][:], in_=vid_pairs[a])
 
-        def load_weights(s):
-            for g in range(PASSES):
+        def load_weights(s, passes=range(PASSES)):
+            for g in passes:
                 nc.sync.dma_start(out=w_raw[s][g][:], in_=w_rows[g, :, :, s * PART_COLS : (s + 1) * PART_COLS])
 
         with tc.manual_schedule():
+            load_weights(PART_ORDER[0], [0])
             load_vid(0)
             nc.sync.dma_start(out=rows[0:1, 0:N_OUT], in_=bias.unsqueeze(0))
             nc.sync.dma_start(out=rows[0:1, N_OUT : N_OUT + HD], in_=q_gain.unsqueeze(0))
             nc.sync.dma_start(out=rows[0:1, N_OUT + HD : ROW_COLS], in_=k_gain.unsqueeze(0))
-            load_weights(PART_ORDER[0])
+            load_weights(PART_ORDER[0], range(1, PASSES))
             for a in range(1, PAIRS):
                 load_vid(a)
             load_weights(PART_ORDER[1])
@@ -86,15 +89,23 @@ def tile_naswinattention_pa_kernel(tc, vid, w_qkv, bias, q_gain, k_gain, out_q, 
         nc.vector.memset(ones[:], 1.0)
         eps = consts.tile([P, 1], F32)
         nc.vector.memset(eps[:], EPS)
+        warm = consts.tile([P, 1], F32)
+        nc.scalar.activation(out=warm[:], in_=eps[:], func=ACT.Abs_reciprocal_sqrt, scale=1.0 / HD, bias=eps[:])
 
-        spread = consts.tile([P, ROW_COLS], BF16)
+        spread = consts.tile([P, N_OUT], BF16)
 
-        def spread_columns(first, width, copy):
+        gains = psum_gain.tile([P, 2 * HD], F32)
+
+        last_gain = consts.tile([P, HD], F32)
+
+        def spread_gains():
+            nc.tensor.matmul(out=gains[:], lhsT=ones[:], rhs=rows[:, N_OUT:ROW_COLS], start=True, stop=True)
+            nc.scalar.copy(out=last_gain[:], in_=gains[:, PART_ORDER[-1] * HD : (PART_ORDER[-1] + 1) * HD])
+
+        def spread_columns(first, copy):
             summed = psum_acc.tile([P, BANK], F32, tag="acc")
-            nc.tensor.matmul(
-                out=summed[:, :width], lhsT=ones[:], rhs=rows[:, first : first + width], start=True, stop=True
-            )
-            copy(out=spread[:, first : first + width], in_=summed[:, :width])
+            nc.tensor.matmul(out=summed[:], lhsT=ones[:], rhs=rows[:, first : first + BANK], start=True, stop=True)
+            copy(out=spread[:, first : first + BANK], in_=summed[:])
 
         v_codes = [keep.tile([P, PAIRS, WINDOWS, P], U32, name="v_codes%d" % g, align_bytes=64) for g in range(PASSES)]
         v_scales = [keep.tile([P, PAIRS, WINDOWS, P], U8, name="v_scales%d" % g, align_bytes=64) for g in range(PASSES)]
@@ -130,7 +141,8 @@ def tile_naswinattention_pa_kernel(tc, vid, w_qkv, bias, q_gain, k_gain, out_q, 
 
         def quantise_weights(s, g, h):
             cols = slice(h * BANK, (h + 1) * BANK)
-            copy = nc.vector.tensor_copy if (s != PART_ORDER[-1] and h == 0) else nc.scalar.copy
+            by_vector = h == 0 and (s == PART_ORDER[0] or (s == PART_ORDER[1] and g < 2))
+            copy = nc.vector.tensor_copy if by_vector else nc.scalar.copy
             grouped_w = stage_w.tile([P, BANK, PACK], BF16, align_bytes=64)
             copy(
                 out=grouped_w[:].rearrange("p (c i) t -> p c t i", i=4),
@@ -160,7 +172,7 @@ def tile_naswinattention_pa_kernel(tc, vid, w_qkv, bias, q_gain, k_gain, out_q, 
                 first = s * PART_COLS + h * BANK
                 nc.vector.tensor_tensor(out=y[:, cols], in0=acc[:], in1=spread[:, first : first + BANK], op=ALU.add)
                 if s < 2:
-                    gain = spread[:, N_OUT + s * HD : N_OUT + (s + 1) * HD]
+                    gain = gains[:, s * HD : (s + 1) * HD]
                     heads = [slice(c0, c0 + HD) for c0 in range(h * BANK, (h + 1) * BANK, HD)]
                     squares = scratch.tile([P, BANK], BF16)
                     sum_sq = stats.tile([P, len(heads)], F32)
@@ -175,7 +187,22 @@ def tile_naswinattention_pa_kernel(tc, vid, w_qkv, bias, q_gain, k_gain, out_q, 
                     nc.scalar.activation(
                         out=rstd[:], in_=sum_sq[:], func=ACT.Abs_reciprocal_sqrt, scale=1.0 / HD, bias=eps[:]
                     )
-                    for i, head in enumerate(heads):
+                    shared = SHARED_HEADS if s == PART_ORDER[-1] else 0
+                    if shared:
+                        last = slice((h + 1) * BANK - shared * HD, (h + 1) * BANK)
+                        z = scratch.tile([P, shared, HD], F32)
+                        nc.gpsimd.tensor_tensor(
+                            out=z[:],
+                            in0=y[:, last].rearrange("p (i d) -> p i d", d=HD),
+                            in1=last_gain[:].unsqueeze(1).to_broadcast([P, shared, HD]),
+                            op=ALU.mult,
+                        )
+                        for j in range(shared):
+                            i = len(heads) - shared + j
+                            nc.scalar.activation(
+                                out=y[:, heads[i]], in_=z[:, j], func=ACT.Copy, scale=rstd[:, i : i + 1]
+                            )
+                    for i, head in enumerate(heads[: len(heads) - shared]):
                         nc.vector.scalar_tensor_tensor(
                             out=y[:, head],
                             in0=y[:, head],
@@ -189,12 +216,12 @@ def tile_naswinattention_pa_kernel(tc, vid, w_qkv, bias, q_gain, k_gain, out_q, 
         units = [(g, h) for g in range(PASSES) for h in range(HALVES)]
         tiles = [(a, n) for a in range(PAIRS) for n in range(WINDOWS)]
 
-        spread_columns(N_OUT, 2 * HD, nc.vector.tensor_copy)
-        for h in range(HALVES):
-            spread_columns(PART_ORDER[0] * PART_COLS + h * BANK, BANK, nc.vector.tensor_copy)
         quantise_tokens(0)
         for g, h in units:
             quantise_weights(PART_ORDER[0], g, h)
+        spread_gains()
+        for h in range(HALVES):
+            spread_columns(PART_ORDER[0] * PART_COLS + h * BANK, nc.vector.tensor_copy)
         for a in range(1, PAIRS):
             quantise_tokens(a)
         for turn, s in enumerate(PART_ORDER):
@@ -204,5 +231,5 @@ def tile_naswinattention_pa_kernel(tc, vid, w_qkv, bias, q_gain, k_gain, out_q, 
                     quantise_weights(PART_ORDER[turn + 1], g, h)
                 elif turn + 1 < PARTS:
                     h = i - len(units)
-                    spread_columns(PART_ORDER[turn + 1] * PART_COLS + h * BANK, BANK, nc.scalar.copy)
+                    spread_columns(PART_ORDER[turn + 1] * PART_COLS + h * BANK, nc.scalar.copy)
                 project(s, a, n)

@@ -100,6 +100,8 @@ def tile_naswinattention_pa_kernel(tc, vid, w_qkv, bias, q_gain, k_gain, out_q, 
 
         def spread_gains():
             nc.tensor.matmul(out=gains[:], lhsT=ones[:], rhs=rows[:, N_OUT:ROW_COLS], start=True, stop=True)
+
+        def copy_last_gain():
             nc.scalar.copy(out=last_gain[:], in_=gains[:, PART_ORDER[-1] * HD : (PART_ORDER[-1] + 1) * HD])
 
         def spread_columns(first, copy):
@@ -211,20 +213,27 @@ def tile_naswinattention_pa_kernel(tc, vid, w_qkv, bias, q_gain, k_gain, out_q, 
                             op0=ALU.mult,
                             op1=ALU.mult,
                         )
-            nc.sync.dma_start(out=outs[s][n, a * P : (a + 1) * P].rearrange("p h d -> p (h d)"), in_=y[:])
+            last = s == PART_ORDER[-1] and (a, n) == (PAIRS - 1, WINDOWS - 1)
+            width = BANK if last else PART_COLS
+            rows_out = outs[s][n, a * P : (a + 1) * P].rearrange("p h d -> p (h d)")
+            for c in range(0, PART_COLS, width):
+                nc.sync.dma_start(out=rows_out[:, c : c + width], in_=y[:, c : c + width])
 
         units = [(g, h) for g in range(PASSES) for h in range(HALVES)]
         tiles = [(a, n) for a in range(PAIRS) for n in range(WINDOWS)]
 
-        quantise_tokens(0)
+        with tc.manual_schedule(engines={mybir.EngineType.PE}):
+            quantise_tokens(0)
+            spread_gains()
+            for h in range(HALVES):
+                spread_columns(PART_ORDER[0] * PART_COLS + h * BANK, nc.vector.tensor_copy)
         for g, h in units:
             quantise_weights(PART_ORDER[0], g, h)
-        spread_gains()
-        for h in range(HALVES):
-            spread_columns(PART_ORDER[0] * PART_COLS + h * BANK, nc.vector.tensor_copy)
         for a in range(1, PAIRS):
             quantise_tokens(a)
         for turn, s in enumerate(PART_ORDER):
+            if s == PART_ORDER[1]:
+                copy_last_gain()
             for i, (a, n) in enumerate(tiles):
                 if turn + 1 < PARTS and i < len(units):
                     g, h = units[i]

from contextlib import ExitStack

import concourse.mybir as mybir
from concourse.masks import make_identity

F32 = mybir.dt.float32
BF16 = mybir.dt.bfloat16
I32 = mybir.dt.int32
U32 = mybir.dt.uint32
U8 = mybir.dt.uint8
FP8X4 = mybir.dt.float8_e4m3fn_x4
ACT = mybir.ActivationFunctionType
ALU = mybir.AluOpType

P = 128
PACK = 4
K_PASS = P * PACK
BANK = 512

TOKENS = 1024
K = 1536
PASSES = K // K_PASS
PARTS = 3
PART_ORDER = (0, 2, 1)
HEADS = 8
HD = 128
PART_COLS = HEADS * HD
N_OUT = PARTS * PART_COLS
HALVES = PART_COLS // BANK
WINDOWS = 2
WIN_W = 8
PAIRS = TOKENS // (2 * P)
EPS = 1e-6
SHARED_HEADS = 1
ROW_COLS = N_OUT + 2 * HD

FLOPS = 2 * TOKENS * K * N_OUT


def tile_naswinattention_pa_kernel(tc, vid, w_qkv, bias, q_gain, k_gain, out_q, out_k, out_v):
    nc = tc.nc
    outs = (out_q, out_k, out_v)

    with ExitStack() as ctx:
        consts = ctx.enter_context(tc.tile_pool(name="consts", bufs=1))
        keep = ctx.enter_context(tc.tile_pool(name="keep", bufs=1))
        stage_v = ctx.enter_context(tc.tile_pool(name="stage_v", bufs=2))
        stage_w = ctx.enter_context(tc.tile_pool(name="stage_w", bufs=4))
        results = ctx.enter_context(tc.tile_pool(name="results", bufs=6))
        scratch = ctx.enter_context(tc.tile_pool(name="scratch", bufs=4))
        stats = ctx.enter_context(tc.tile_pool(name="stats", bufs=8))
        psum_t = ctx.enter_context(tc.psum_pool(name="psum_t", bufs=2))
        psum_acc = ctx.enter_context(tc.psum_pool(name="psum_acc", bufs=5))
        psum_gain = ctx.enter_context(tc.psum_pool(name="psum_gain", bufs=1))

        rows = consts.tile([P, ROW_COLS], BF16)
        nc.vector.memset(rows[:].bitcast(I32), 0)

        vid_pairs = vid.rearrange("(a j p) k -> a p j k", j=2, p=P)
        vid_sb = [keep.tile([P, 2, K], BF16, name="vid_sb%d" % a) for a in range(PAIRS)]
        w_rows = w_qkv.rearrange("(g p t) c -> g p t c", p=P, t=PACK)
        w_raw = [
            [keep.tile([P, PACK, PART_COLS], BF16, name="w_raw%d_%d" % (s, g)) for g in range(PASSES)]
            for s in range(PARTS)
        ]

        def load_vid(a):
            nc.sync.dma_start(out=vid_sb[a][:], in_=vid_pairs[a])

        def load_weights(s, passes=range(PASSES)):
            for g in passes:
                nc.sync.dma_start(out=w_raw[s][g][:], in_=w_rows[g, :, :, s * PART_COLS : (s + 1) * PART_COLS])

        with tc.manual_schedule():
            load_weights(PART_ORDER[0], [0])
            load_vid(0)
            nc.sync.dma_start(out=rows[0:1, 0:N_OUT], in_=bias.unsqueeze(0))
            nc.sync.dma_start(out=rows[0:1, N_OUT : N_OUT + HD], in_=q_gain.unsqueeze(0))
            nc.sync.dma_start(out=rows[0:1, N_OUT + HD : ROW_COLS], in_=k_gain.unsqueeze(0))
            load_weights(PART_ORDER[0], range(1, PASSES))
            for a in range(1, PAIRS):
                load_vid(a)
            load_weights(PART_ORDER[1])
            load_weights(PART_ORDER[2])

        ident = consts.tile([P, P], F32)
        make_identity(nc, ident[:])
        ones = consts.tile([P, P], BF16)
        nc.vector.memset(ones[:], 1.0)
        eps = consts.tile([P, 1], F32)
        nc.vector.memset(eps[:], EPS)
        warm = consts.tile([P, 1], F32)
        nc.scalar.activation(out=warm[:], in_=eps[:], func=ACT.Abs_reciprocal_sqrt, scale=1.0 / HD, bias=eps[:])

        spread = consts.tile([P, N_OUT], BF16)

        gains = psum_gain.tile([P, 2 * HD], F32)

        last_gain = consts.tile([P, HD], F32)

        def spread_gains():
            nc.tensor.matmul(out=gains[:], lhsT=ones[:], rhs=rows[:, N_OUT:ROW_COLS], start=True, stop=True)

        def copy_last_gain():
            nc.scalar.copy(out=last_gain[:], in_=gains[:, PART_ORDER[-1] * HD : (PART_ORDER[-1] + 1) * HD])

        def spread_columns(first, copy):
            summed = psum_acc.tile([P, BANK], F32, tag="acc")
            nc.tensor.matmul(out=summed[:], lhsT=ones[:], rhs=rows[:, first : first + BANK], start=True, stop=True)
            copy(out=spread[:, first : first + BANK], in_=summed[:])

        v_codes = [keep.tile([P, PAIRS, WINDOWS, P], U32, name="v_codes%d" % g, align_bytes=64) for g in range(PASSES)]
        v_scales = [keep.tile([P, PAIRS, WINDOWS, P], U8, name="v_scales%d" % g, align_bytes=64) for g in range(PASSES)]

        def quantise_tokens(a):
            words = vid_sb[a][:].bitcast(F32)
            grouped_v = stage_v.tile([P, PASSES, WINDOWS, P * PACK], BF16, align_bytes=64)
            grouped_words = grouped_v[:].bitcast(F32)
            for g in range(PASSES):
                flipped = psum_t.tile([P, 2, 2 * P], F32)
                for u in range(2):
                    for j in range(2):
                        nc.tensor.transpose(
                            flipped[:, u, j * P : (j + 1) * P],
                            words[:, j, 2 * P * g + u : 2 * P * (g + 1) : 2],
                            ident[:],
                        )
                by_window = flipped[:].rearrange("p u (s n w) -> p n s w u", n=WINDOWS, w=WIN_W)
                for n in range(WINDOWS):
                    nc.scalar.copy(
                        out=grouped_words[:, g, n, :].rearrange("p (s w u) -> p s w u", w=WIN_W, u=2),
                        in_=by_window[:, n],
                    )
            for g in range(PASSES):
                nc.vector.quantize_mx(
                    out=v_codes[g][:, a].rearrange("p n c -> p (n c)").bitcast(FP8X4),
                    scales=v_scales[g][:, a].rearrange("p n c -> p (n c)"),
                    in_=grouped_v[:, g].rearrange("p n c -> p (n c)"),
                )

        w_codes = [keep.tile([P, PASSES, PART_COLS], U32, name="w_codes%d" % s, align_bytes=64) for s in range(PARTS)]
        w_scales = [keep.tile([P, PASSES, PART_COLS], U8, name="w_scales%d" % s, align_bytes=64) for s in range(PARTS)]

        def quantise_weights(s, g, h):
            cols = slice(h * BANK, (h + 1) * BANK)
            by_vector = h == 0 and (s == PART_ORDER[0] or (s == PART_ORDER[1] and g < 2))
            copy = nc.vector.tensor_copy if by_vector else nc.scalar.copy
            grouped_w = stage_w.tile([P, BANK, PACK], BF16, align_bytes=64)
            copy(
                out=grouped_w[:].rearrange("p (c i) t -> p c t i", i=4),
                in_=w_raw[s][g][:, :, cols].rearrange("p t (c i) -> p c t i", i=4),
            )
            nc.vector.quantize_mx(
                out=w_codes[s][:, g, cols].bitcast(FP8X4),
                scales=w_scales[s][:, g, cols],
                in_=grouped_w[:].rearrange("p c t -> p (c t)"),
            )

        def project(s, a, n):
            y = results.tile([P, PART_COLS], F32)
            for h in range(HALVES):
                cols = slice(h * BANK, (h + 1) * BANK)
                acc = psum_acc.tile([P, BANK], F32, tag="acc")
                for g in range(PASSES):
                    nc.tensor.matmul_mx(
                        out=acc[:],
                        lhsT=v_codes[g][:, a, n, :].bitcast(FP8X4),
                        lhsT_scale=v_scales[g][:, a, n, :],
                        rhs=w_codes[s][:, g, cols].bitcast(FP8X4),
                        rhs_scale=w_scales[s][:, g, cols],
                        start=(g == 0),
                        stop=(g == PASSES - 1),
                    )
                first = s * PART_COLS + h * BANK
                nc.vector.tensor_tensor(out=y[:, cols], in0=acc[:], in1=spread[:, first : first + BANK], op=ALU.add)
                if s < 2:
                    gain = gains[:, s * HD : (s + 1) * HD]
                    heads = [slice(c0, c0 + HD) for c0 in range(h * BANK, (h + 1) * BANK, HD)]
                    squares = scratch.tile([P, BANK], BF16)
                    sum_sq = stats.tile([P, len(heads)], F32)
                    for i, head in enumerate(heads):
                        nc.scalar.activation(
                            out=squares[:, i * HD : (i + 1) * HD],
                            in_=y[:, head],
                            func=ACT.Square,
                            accum_out=sum_sq[:, i : i + 1],
                        )
                    rstd = stats.tile([P, len(heads)], F32)
                    nc.scalar.activation(
                        out=rstd[:], in_=sum_sq[:], func=ACT.Abs_reciprocal_sqrt, scale=1.0 / HD, bias=eps[:]
                    )
                    shared = SHARED_HEADS if s == PART_ORDER[-1] else 0
                    if shared:
                        last = slice((h + 1) * BANK - shared * HD, (h + 1) * BANK)
                        z = scratch.tile([P, shared, HD], F32)
                        nc.gpsimd.tensor_tensor(
                            out=z[:],
                            in0=y[:, last].rearrange("p (i d) -> p i d", d=HD),
                            in1=last_gain[:].unsqueeze(1).to_broadcast([P, shared, HD]),
                            op=ALU.mult,
                        )
                        for j in range(shared):
                            i = len(heads) - shared + j
                            nc.scalar.activation(
                                out=y[:, heads[i]], in_=z[:, j], func=ACT.Copy, scale=rstd[:, i : i + 1]
                            )
                    for i, head in enumerate(heads[: len(heads) - shared]):
                        nc.vector.scalar_tensor_tensor(
                            out=y[:, head],
                            in0=y[:, head],
                            scalar=rstd[:, i : i + 1],
                            in1=gain,
                            op0=ALU.mult,
                            op1=ALU.mult,
                        )
            last = s == PART_ORDER[-1] and (a, n) == (PAIRS - 1, WINDOWS - 1)
            width = BANK if last else PART_COLS
            rows_out = outs[s][n, a * P : (a + 1) * P].rearrange("p h d -> p (h d)")
            for c in range(0, PART_COLS, width):
                nc.sync.dma_start(out=rows_out[:, c : c + width], in_=y[:, c : c + width])

        units = [(g, h) for g in range(PASSES) for h in range(HALVES)]
        tiles = [(a, n) for a in range(PAIRS) for n in range(WINDOWS)]

        with tc.manual_schedule(engines={mybir.EngineType.PE}):
            quantise_tokens(0)
            spread_gains()
            for h in range(HALVES):
                spread_columns(PART_ORDER[0] * PART_COLS + h * BANK, nc.vector.tensor_copy)
        for g, h in units:
            quantise_weights(PART_ORDER[0], g, h)
        for a in range(1, PAIRS):
            quantise_tokens(a)
        for turn, s in enumerate(PART_ORDER):
            if s == PART_ORDER[1]:
                copy_last_gain()
            for i, (a, n) in enumerate(tiles):
                if turn + 1 < PARTS and i < len(units):
                    g, h = units[i]
                    quantise_weights(PART_ORDER[turn + 1], g, h)
                elif turn + 1 < PARTS:
                    h = i - len(units)
                    spread_columns(PART_ORDER[turn + 1] * PART_COLS + h * BANK, nc.scalar.copy)
                project(s, a, n)
